import numpy as np
import ml_dtypes


def mxq(x, axis, fmt="e4m3"):
    dtype, down = {"e4m3": (ml_dtypes.float8_e4m3fn, 7), "e5m2": (ml_dtypes.float8_e5m2, 14)}[fmt]
    v = np.moveaxis(np.asarray(x, np.float32).astype(ml_dtypes.bfloat16).astype(np.float64), axis, -1)
    blocks = v.reshape(v.shape[:-1] + (-1, 32))
    amax = np.abs(blocks).max(-1, keepdims=True)
    byte = np.maximum(np.where(amax > 0, np.frexp(amax)[1] - 1 + 127, 0) - down, 1)
    scale = np.exp2(byte - 127.0)
    codes = (blocks / scale).astype(np.float32).astype(dtype).astype(np.float64)
    return np.moveaxis((codes * scale).reshape(v.shape), -1, axis)


WIDE = False


def mx_kscale(k):
    if not WIDE:
        return np.ones(k)
    levels = np.array([10, -10, 5, -5, 0])
    if k % 512:
        return np.exp2(np.random.permutation(np.resize(levels, k // 32))).repeat(32)
    a = np.empty((k // 512, 16))
    for p in range(k // 512):
        a[p, :8] = np.random.permutation(np.resize(levels, 8))
        for g in range(8):
            far = levels[np.abs(levels - a[p, g]) >= 10]
            a[p, g + 8] = far[np.random.randint(len(far))]
    return np.exp2(a.ravel()).repeat(32)


BF16 = ml_dtypes.bfloat16


def bf(x):
    return np.asarray(x, np.float32).astype(BF16)


def f64(x):
    return np.asarray(x).astype(np.float64)


C, H, W, CO, G = 128, 64, 64, 256, 128
K = 4 * C
P = (H // 2) * (W // 2)
EPS = 1e-5


def haar_bands(x):
    xr = x.reshape(C, H // 2, 2, W // 2, 2)
    x00 = xr[:, :, 0, :, 0]
    x01 = xr[:, :, 0, :, 1]
    x10 = xr[:, :, 1, :, 0]
    x11 = xr[:, :, 1, :, 1]
    half = 0.5
    LL = (x00 + x01 + x10 + x11) * half
    HL = (-x00 - x01 + x10 + x11) * half
    LH = (-x00 + x01 - x10 + x11) * half
    HH = (x00 - x01 - x10 + x11) * half
    return LL, HL, LH, HH


def group_norm(y, scale, bias, groups):
    c, h, w = y.shape
    yg = y.reshape(groups, c // groups, h, w)
    mean = np.mean(yg, axis=(1, 2, 3), keepdims=True)
    var = np.mean(np.square(yg - mean), axis=(1, 2, 3), keepdims=True)
    yn = ((yg - mean) / np.sqrt(var + EPS)).reshape(c, h, w)
    return yn * scale[:, None, None] + bias[:, None, None]


def setup_inputs():
    s = mx_kscale(K)
    return {"x": bf(np.random.standard_normal((C, H, W))),
            "gn_scale": bf((1.0 + 0.1 * np.random.standard_normal(K)) * s),
            "gn_bias": bf(0.1 * np.random.standard_normal(K) * s),
            "w_proj": bf(np.random.standard_normal((CO, K)) / np.sqrt(K) / s[None, :])}


def reference(x, gn_scale, gn_bias, w_proj):
    LL, HL, LH, HH = haar_bands(f64(x))
    y = np.concatenate([LL, HL, LH, HH], axis=0)
    y = group_norm(y, f64(gn_scale), f64(gn_bias), G)
    z = mxq(f64(w_proj), 1, "e4m3") @ mxq(y.reshape(K, P), 0, "e4m3")
    return np.maximum(z, 0.0).reshape(CO, H // 2, W // 2)

@@ -1,0 +1,359 @@
+from contextlib import ExitStack
+
+import concourse.mybir as mybir
+from concourse.masks import make_identity
+
+F32 = mybir.dt.float32
+BF16 = mybir.dt.bfloat16
+I32 = mybir.dt.int32
+U8 = mybir.dt.uint8
+FP8X4 = mybir.dt.float8_e4m3fn_x4
+ALU = mybir.AluOpType
+ACT = mybir.ActivationFunctionType
+
+P = 128
+C = 128
+H = 64
+W = 64
+T = 4
+Q = C // T
+S = 2
+R = 2
+K = 2
+HALF_ROWS = H // S
+HALF_W = W // 2
+PIX = (HALF_ROWS // 2) * HALF_W
+CO = 256
+M_TILES = CO // P
+EPS = 1e-5
+
+CHUNK_ROWS = (4, 8, 12, 8)
+PIECES = ((0, 0, 2), (1, 0, 4), (2, 0, 6), (3, 0, 2), (3, 2, 4))
+N_TILES = 4
+N_PIX = PIX // N_TILES
+NORM_PIECES = 2
+NORM_PIX = PIX // NORM_PIECES
+RUN = 4
+
+EPS_UNHALVED = 4.0 * EPS
+
+FLOPS = 2 * CO * 4 * C * S * PIX
+
+
+def tile_hwdconv_s_kernel(tc, x, gn_scale, gn_bias, w_proj, out):
+    nc = tc.nc
+    with ExitStack() as ctx:
+        keep = ctx.enter_context(tc.tile_pool(name="keep", bufs=1))
+        psum = ctx.enter_context(tc.psum_pool(name="psum", bufs=1))
+        ctx.enter_context(tc.manual_schedule())
+
+        x_dram = x.rearrange("(q t) (s h) w -> s q t (h w)", t=T, s=S)
+        w_sb = keep.tile([P, M_TILES, 3 * R * C], BF16)
+        w_dram = w_proj.rearrange("(m o) c -> o m c", o=P)
+        bounds = [0]
+        for rows in CHUNK_ROWS:
+            bounds.append(bounds[-1] + rows)
+        chunks = list(zip(bounds[:-1], bounds[1:]))
+        x_sb = [
+            keep.tile([P, T, rows // 2, 2, W], BF16, name="x_sb%d" % i)
+            for i, rows in enumerate(CHUNK_ROWS)
+        ]
+        for i, (row0, row1) in enumerate(chunks):
+            cols = slice(row0 * W, row1 * W)
+            x_flat = x_sb[i][:].rearrange("p t i a w -> p t (i a w)")
+            for s in range(S):
+                queue = nc.scalar if s == 1 and i < 2 else nc.sync
+                for r in range(R):
+                    p0 = (s * R + r) * Q
+                    queue.dma_start(out=x_flat[p0 : p0 + Q, :, :], in_=x_dram[s][:, :, cols])
+        gn_rows = keep.tile([P, S, R * C], BF16)
+        nc.vector.memset(gn_rows[:], 0.0)
+        ident = keep.tile([P, P], BF16)
+        make_identity(nc, ident[:])
+        nc.gpsimd.dma_start(out=w_sb[:, :, 0 : 2 * R * C], in_=w_dram)
+        nc.gpsimd.dma_start(out=w_sb[:, :, 2 * R * C : 3 * R * C], in_=w_dram[:, :, 0 : R * C])
+        for i, vec in enumerate((gn_scale, gn_bias)):
+            nc.gpsimd.dma_start(
+                out=gn_rows[i * K : (i + 1) * K, :, :],
+                in_=vec.rearrange("(k c) -> k c", k=K).unsqueeze(1).to_broadcast([K, S, R * C]),
+            )
+
+        row_sign = keep.tile([P, 1], F32)
+        nc.vector.memset(row_sign[:], 1.0)
+        for s in range(S):
+            p0 = (s * R + 1) * Q
+            nc.vector.memset(row_sign[p0 : p0 + Q, :], -1.0)
+        table_warm = keep.tile([P, 1], F32)
+        nc.scalar.activation(out=table_warm[:], in_=row_sign[:], func=ACT.Abs_reciprocal_sqrt)
+
+        w_codes = [
+            keep.tile([P, K, CO], I32, align_bytes=64, name="w_codes%d" % s) for s in range(S)
+        ]
+        for s in range(S):
+            p0 = (1 - s) * (P // S)
+            nc.vector.memset(w_codes[s][p0 : p0 + P // S, :, :], 0)
+
+        pair_half = keep.tile([P, P // S], F32)
+        nc.vector.tensor_tensor(
+            out=pair_half[:], in0=ident[:, 0 : P // S], in1=ident[:, P // S : P], op=ALU.add
+        )
+        pair = keep.tile([P, S, P // S], F32)
+        nc.vector.tensor_scalar(
+            out=pair[:],
+            in0=pair_half[:].unsqueeze(1).to_broadcast([P, S, P // S]),
+            scalar1=1.0 / (T * S * PIX),
+            scalar2=None,
+            op0=ALU.mult,
+        )
+        pair_2d = pair[:].rearrange("p s j -> p (s j)")
+
+        u = [
+            keep.tile([P, T * (rows // 2), HALF_W, 2], F32, name="u%d" % i)
+            for i, rows in enumerate(CHUNK_ROWS)
+        ]
+        bands = keep.tile([P, K, T, PIX], F32)
+        squares_scrap = keep.tile([P, K, T, PIX], BF16)
+        sums = keep.tile([P, len(PIECES), K], F32)
+        sumsq = keep.tile([P, len(PIECES), K], F32)
+        mean_ps = psum.tile([P, K], F32, tag="mean", name="mean_ps")
+        meansq_ps = psum.tile([P, K], F32, name="meansq_ps")
+        shift = keep.tile([P, K], F32)
+
+        def haar_rows(i):
+            rows = x_sb[i][:].rearrange("p t i a w -> p (t i) a w")
+            nc.vector.scalar_tensor_tensor(
+                out=u[i][:].rearrange("p i j b -> p i (j b)"),
+                in0=rows[:, :, 0, :],
+                scalar=row_sign[:, 0:1],
+                in1=rows[:, :, 1, :],
+                op0=ALU.mult,
+                op1=ALU.add,
+            )
+
+        def piece_pixels(n):
+            i, pair0, pair1 = PIECES[n]
+            base = chunks[i][0] // 2
+            return slice((base + pair0) * HALF_W, (base + pair1) * HALF_W)
+
+        def haar_cols(n):
+            i, pair0, pair1 = PIECES[n]
+            u_px = u[i][:].rearrange("p (t i) j b -> p t (i j) b", t=T)
+            u_px = u_px[:, :, pair0 * HALF_W : pair1 * HALF_W, :]
+            px = piece_pixels(n)
+            for k in range(K):
+                nc.vector.scalar_tensor_tensor(
+                    out=bands[:, k, :, px],
+                    in0=u_px[:, :, :, 1],
+                    scalar=shift[:, k : k + 1],
+                    in1=u_px[:, :, :, 0],
+                    op0=ALU.subtract,
+                    op1=ALU.subtract if k else ALU.add,
+                    accum_out=sums[:, n, k : k + 1],
+                )
+
+        def square(n):
+            px = piece_pixels(n)
+            for k in range(K):
+                nc.scalar.activation(
+                    out=squares_scrap[:, k, :, px],
+                    in_=bands[:, k, :, px],
+                    func=ACT.Square,
+                    accum_out=sumsq[:, n, k : k + 1],
+                )
+
+        def add_up(total_ps, parts, n):
+            nc.tensor.matmul(
+                out=total_ps[:], lhsT=pair_2d, rhs=parts[:, n, :],
+                start=n == 0, stop=n == len(PIECES) - 1,
+            )
+
+        haar_rows(0)
+        est_rows = T * CHUNK_ROWS[0] // 2
+        est = keep.tile([P, 3], F32)
+        est_scrap = keep.tile([P, 3, est_rows, HALF_W], BF16)
+        for n, (b, sign) in enumerate(((1, 1.0), (0, 1.0), (0, -1.0))):
+            nc.scalar.activation(
+                out=est_scrap[:, n, :, :],
+                in_=u[0][:, :, :, b],
+                func=ACT.Copy,
+                scale=sign,
+                accum_out=est[:, n : n + 1],
+            )
+        shift_ps = psum.tile([P, K], F32, tag="mean", name="shift_ps")
+        nc.tensor.matmul(
+            out=shift_ps[:], lhsT=pair_2d, rhs=est[:, 0:1].to_broadcast([P, K]),
+            start=True, stop=False,
+        )
+        nc.tensor.matmul(out=shift_ps[:], lhsT=pair_2d, rhs=est[:, 1:3], start=False, stop=True)
+        nc.scalar.mul(out=shift[:], in_=shift_ps[:], mul=float(HALF_ROWS // chunks[0][1]))
+
+        haar_rows(1)
+
+        w_grouped = keep.tile([P, K, M_TILES, P, T], BF16, align_bytes=64)
+        w_t = [
+            psum.tile([P, M_TILES, T, P], BF16, tag="acc%d" % (4 + n), name="w_t%d" % n)
+            for n in range(K)
+        ]
+        for n in range(K):
+            for m in range(M_TILES):
+                for t in range(T):
+                    c0 = n * R * C + t
+                    nc.tensor.transpose(
+                        w_t[n][:, m, t, :], w_sb[:, m, c0 : c0 + T * (P - 1) + 1 : T], ident[:]
+                    )
+
+        def gather_w(n):
+            nc.scalar.copy(
+                out=w_grouped[:, n, :, :, :], in_=w_t[n][:].rearrange("p m t o -> p m o t")
+            )
+
+        gather_w(0)
+        haar_cols(0)
+        square(0)
+        gather_w(1)
+        add_up(mean_ps, sums, 0)
+        add_up(meansq_ps, sumsq, 0)
+
+        haar_rows(2)
+        haar_cols(1)
+        square(1)
+        add_up(mean_ps, sums, 1)
+        add_up(meansq_ps, sumsq, 1)
+        gn_t = psum.tile([P, T, P], BF16, tag="acc3", name="gn_t")
+        gn_flat = gn_rows[:].rearrange("p s c -> p (s c)")
+        for t in range(T):
+            nc.tensor.transpose(gn_t[:, t, :], gn_flat[:, t : t + T * (P - 1) + 1 : T], ident[:])
+        gain = keep.tile([P, K, T], F32)
+        bias = keep.tile([P, K, T], F32)
+        nc.scalar.copy(out=gain[:], in_=gn_t[:, :, 0:K].rearrange("p t k -> p k t"))
+        nc.scalar.copy(out=bias[:], in_=gn_t[:, :, K : 2 * K].rearrange("p t k -> p k t"))
+        haar_rows(3)
+        haar_cols(2)
+        square(2)
+        add_up(mean_ps, sums, 2)
+        add_up(meansq_ps, sumsq, 2)
+        for n in (3, 4):
+            haar_cols(n)
+            square(n)
+            add_up(mean_ps, sums, n)
+        for n in (3, 4):
+            add_up(meansq_ps, sumsq, n)
+
+        w_all = keep.tile([P, K, CO], I32, align_bytes=64)
+        w_scales = keep.tile([P, K, CO], U8, align_bytes=64)
+        nc.vector.quantize_mx(
+            out=w_all[:].rearrange("p n o -> p (n o)").bitcast(FP8X4),
+            scales=w_scales[:].rearrange("p n o -> p (n o)"),
+            in_=w_grouped[:].rearrange("p n m o t -> p (n m o t)"),
+        )
+
+        mean = keep.tile([P, K], F32)
+        nc.vector.tensor_copy(out=mean[:], in_=mean_ps[:])
+        pull = keep.tile([P, K, T], F32)
+        nc.vector.scalar_tensor_tensor(
+            out=pull[:],
+            in0=gain[:],
+            scalar=-1.0,
+            in1=mean[:].unsqueeze(2).to_broadcast([P, K, T]),
+            op0=ALU.mult,
+            op1=ALU.mult,
+        )
+        mean_squared = keep.tile([P, K], F32)
+        nc.vector.tensor_tensor(out=mean_squared[:], in0=mean[:], in1=mean[:], op=ALU.mult)
+        eps_pull = keep.tile([P, K], F32)
+        nc.vector.tensor_scalar(
+            out=eps_pull[:], in0=mean_squared[:],
+            scalar1=-1.0, scalar2=EPS_UNHALVED, op0=ALU.mult, op1=ALU.add,
+        )
+        rstd = keep.tile([P, K], F32)
+        slope = keep.tile([P, K, T], F32)
+        offset = keep.tile([P, K, T], F32)
+        nc.vector.tensor_copy(
+            out=w_codes[0][0 : P // S, :, :], in_=w_all[0 : P // S, :, :]
+        )
+        for k in range(K):
+            nc.scalar.activation(
+                out=rstd[:, k : k + 1], in_=meansq_ps[:, k : k + 1],
+                func=ACT.Abs_reciprocal_sqrt, bias=eps_pull[:, k : k + 1],
+            )
+        for k in range(K):
+            nc.vector.tensor_scalar(
+                out=slope[:, k, :], in0=gain[:, k, :],
+                scalar1=rstd[:, k : k + 1], scalar2=None, op0=ALU.mult,
+            )
+            nc.vector.scalar_tensor_tensor(
+                out=offset[:, k, :], in0=pull[:, k, :], scalar=rstd[:, k : k + 1],
+                in1=bias[:, k, :], op0=ALU.mult, op1=ALU.add,
+            )
+
+        y_planar = keep.tile([P, N_TILES, T, K, N_PIX], BF16)
+
+        def normalise(engine, piece, k, t):
+            tiles = slice(piece * NORM_PIX // N_PIX, (piece + 1) * NORM_PIX // N_PIX)
+            src = bands[:, k, t, piece * NORM_PIX : (piece + 1) * NORM_PIX].rearrange(
+                "p (n c) -> p n c", c=N_PIX
+            )
+            slope_t, offset_t = slope[:, k, t : t + 1], offset[:, k, t : t + 1]
+            if engine is nc.scalar:
+                nc.scalar.activation(
+                    out=y_planar[:, tiles, t, k, :], in_=src,
+                    func=ACT.Identity, scale=slope_t, bias=offset_t,
+                )
+            else:
+                nc.vector.tensor_scalar(
+                    out=y_planar[:, tiles, t, k, :], in0=src,
+                    scalar1=slope_t, scalar2=offset_t, op0=ALU.mult, op1=ALU.add,
+                )
+
+        for piece in range(NORM_PIECES):
+            for k in range(K):
+                for t in range(T):
+                    normalise(nc.scalar if t % 2 == 0 else nc.vector, piece, k, t)
+        nc.vector.tensor_copy(
+            out=w_codes[1][P // S : P, :, :], in_=w_all[P // S : P, :, :]
+        )
+
+        y_grouped = keep.tile([P, N_TILES, K, N_PIX, T], BF16, align_bytes=64)
+        y_codes = keep.tile([P, N_TILES, K, N_PIX], I32, align_bytes=64)
+        y_scales = keep.tile([P, N_TILES, K, N_PIX], U8, align_bytes=64)
+        out_dram = out.rearrange("(m o) (s i) j -> m o s (i j)", o=P, s=S)
+
+        def regroup(n):
+            nc.vector.tensor_copy(
+                out=y_grouped[:, n, :, :, :].rearrange("p k (c i) t -> p (k c) t i", i=RUN),
+                in_=y_planar[:, n, :, :, :].rearrange("p t k (c i) -> p (k c) t i", i=RUN),
+            )
+
+        regroup(0)
+        for n in range(N_TILES):
+            px = slice(n * N_PIX, (n + 1) * N_PIX)
+            if n + 1 < N_TILES:
+                regroup(n + 1)
+            nc.vector.quantize_mx(
+                out=y_codes[:, n, :, :].rearrange("p k c -> p (k c)").bitcast(FP8X4),
+                scales=y_scales[:, n, :, :].rearrange("p k c -> p (k c)"),
+                in_=y_grouped[:, n, :, :, :].rearrange("p k c t -> p (k c t)"),
+            )
+            for m in range(M_TILES):
+                acc = psum.tile(
+                    [P, S, N_PIX], F32, tag="acc%d" % ((n * M_TILES + m) % 6), name="acc%d%d" % (n, m)
+                )
+                for s in range(S):
+                    for k in range(K):
+                        col = k if s == 0 else 1 - k
+                        o_cols = slice(m * P, (m + 1) * P)
+                        nc.tensor.matmul_mx(
+                            out=acc[:, s, :],
+                            lhsT=w_codes[s][:, col, o_cols].bitcast(FP8X4),
+                            lhsT_scale=w_scales[:, col, o_cols],
+                            rhs=y_codes[:, n, k, :].bitcast(FP8X4),
+                            rhs_scale=y_scales[:, n, k, :],
+                            start=k == 0,
+                            stop=k == K - 1,
+                        )
+                result = keep.tile([P, S, N_PIX], F32, name="result%d%d" % (n, m))
+                if n == N_TILES - 1 and m == 0:
+                    nc.vector.tensor_scalar_max(out=result[:], in0=acc[:], scalar1=0.0)
+                else:
+                    nc.scalar.activation(out=result[:], in_=acc[:], func=ACT.Relu)
+                nc.sync.dma_start(out=out_dram[m][:, :, px], in_=result[:])

@@ -27,12 +27,13 @@ CO = 256
 M_TILES = CO // P
 EPS = 1e-5
 
-CHUNK_ROWS = (4, 8, 12, 8)
-PIECES = ((0, 0, 2), (1, 0, 4), (2, 0, 6), (3, 0, 2), (3, 2, 4))
+CHUNK_ROWS = (4, 12, 16)
+PIECES = ((0, 0, 2), (1, 0, 6), (2, 0, 4), (2, 4, 7), (2, 7, 8))
 N_TILES = 4
 N_PIX = PIX // N_TILES
 NORM_PIECES = 2
 NORM_PIX = PIX // NORM_PIECES
+WARM_PASSES = 12
 RUN = 4
 
 EPS_UNHALVED = 4.0 * EPS
@@ -48,7 +49,7 @@ def tile_hwdconv_s_kernel(tc, x, gn_scale, gn_bias, w_proj, out):
         ctx.enter_context(tc.manual_schedule())
 
         x_dram = x.rearrange("(q t) (s h) w -> s q t (h w)", t=T, s=S)
-        w_sb = keep.tile([P, M_TILES, 3 * R * C], BF16)
+        w_sb = keep.tile([P, M_TILES, K * R * C], BF16)
         w_dram = w_proj.rearrange("(m o) c -> o m c", o=P)
         bounds = [0]
         for rows in CHUNK_ROWS:
@@ -61,17 +62,16 @@ def tile_hwdconv_s_kernel(tc, x, gn_scale, gn_bias, w_proj, out):
         for i, (row0, row1) in enumerate(chunks):
             cols = slice(row0 * W, row1 * W)
             x_flat = x_sb[i][:].rearrange("p t i a w -> p t (i a w)")
-            for s in range(S):
-                queue = nc.scalar if s == 1 and i < 2 else nc.sync
-                for r in range(R):
+            for r in range(R):
+                for s in range(S):
+                    queue = nc.scalar if s == 1 and i < 2 else nc.sync
                     p0 = (s * R + r) * Q
                     queue.dma_start(out=x_flat[p0 : p0 + Q, :, :], in_=x_dram[s][:, :, cols])
         gn_rows = keep.tile([P, S, R * C], BF16)
         nc.vector.memset(gn_rows[:], 0.0)
         ident = keep.tile([P, P], BF16)
         make_identity(nc, ident[:])
-        nc.gpsimd.dma_start(out=w_sb[:, :, 0 : 2 * R * C], in_=w_dram)
-        nc.gpsimd.dma_start(out=w_sb[:, :, 2 * R * C : 3 * R * C], in_=w_dram[:, :, 0 : R * C])
+        nc.gpsimd.dma_start(out=w_sb[:], in_=w_dram)
         for i, vec in enumerate((gn_scale, gn_bias)):
             nc.gpsimd.dma_start(
                 out=gn_rows[i * K : (i + 1) * K, :, :],
@@ -86,12 +86,13 @@ def tile_hwdconv_s_kernel(tc, x, gn_scale, gn_bias, w_proj, out):
         table_warm = keep.tile([P, 1], F32)
         nc.scalar.activation(out=table_warm[:], in_=row_sign[:], func=ACT.Abs_reciprocal_sqrt)
 
-        w_codes = [
-            keep.tile([P, K, CO], I32, align_bytes=64, name="w_codes%d" % s) for s in range(S)
+        w_mx = [
+            keep.tile([P, K, CO + CO // 4], I32, align_bytes=64, name="w_mx%d" % s)
+            for s in range(S)
         ]
         for s in range(S):
             p0 = (1 - s) * (P // S)
-            nc.vector.memset(w_codes[s][p0 : p0 + P // S, :, :], 0)
+            nc.vector.memset(w_mx[s][p0 : p0 + P // S, :, :], 0)
 
         pair_half = keep.tile([P, P // S], F32)
         nc.vector.tensor_tensor(
@@ -189,36 +190,17 @@ def tile_hwdconv_s_kernel(tc, x, gn_scale, gn_bias, w_proj, out):
 
         haar_rows(1)
 
-        w_grouped = keep.tile([P, K, M_TILES, P, T], BF16, align_bytes=64)
-        w_t = [
-            psum.tile([P, M_TILES, T, P], BF16, tag="acc%d" % (4 + n), name="w_t%d" % n)
-            for n in range(K)
-        ]
-        for n in range(K):
-            for m in range(M_TILES):
-                for t in range(T):
-                    c0 = n * R * C + t
-                    nc.tensor.transpose(
-                        w_t[n][:, m, t, :], w_sb[:, m, c0 : c0 + T * (P - 1) + 1 : T], ident[:]
-                    )
+        w_t = psum.tile([P, M_TILES, T, P], BF16, tag="acc4", name="w_t")
+        for m in range(M_TILES):
+            for t in range(T):
+                nc.tensor.transpose(w_t[:, m, t, :], w_sb[:, m, t : t + T * (P - 1) + 1 : T], ident[:])
+        w_grouped = keep.tile([P, M_TILES, P, T], BF16, align_bytes=64)
+        nc.scalar.copy(out=w_grouped[:], in_=w_t[:].rearrange("p m t o -> p m o t"))
 
-        def gather_w(n):
-            nc.scalar.copy(
-                out=w_grouped[:, n, :, :, :], in_=w_t[n][:].rearrange("p m t o -> p m o t")
-            )
-
-        gather_w(0)
         haar_cols(0)
         square(0)
-        gather_w(1)
-        add_up(mean_ps, sums, 0)
-        add_up(meansq_ps, sumsq, 0)
-
-        haar_rows(2)
         haar_cols(1)
         square(1)
-        add_up(mean_ps, sums, 1)
-        add_up(meansq_ps, sumsq, 1)
         gn_t = psum.tile([P, T, P], BF16, tag="acc3", name="gn_t")
         gn_flat = gn_rows[:].rearrange("p s c -> p (s c)")
         for t in range(T):
@@ -227,25 +209,46 @@ def tile_hwdconv_s_kernel(tc, x, gn_scale, gn_bias, w_proj, out):
         bias = keep.tile([P, K, T], F32)
         nc.scalar.copy(out=gain[:], in_=gn_t[:, :, 0:K].rearrange("p t k -> p k t"))
         nc.scalar.copy(out=bias[:], in_=gn_t[:, :, K : 2 * K].rearrange("p t k -> p k t"))
-        haar_rows(3)
+        for n in (0, 1):
+            add_up(mean_ps, sums, n)
+            add_up(meansq_ps, sumsq, n)
+
+        w_all = keep.tile([P, CO + CO // 4], I32, align_bytes=64)
+        nc.vector.quantize_mx(
+            out=w_all[:, 0:CO].bitcast(FP8X4),
+            scales=w_all[:, CO:].bitcast(U8),
+            in_=w_grouped[:].rearrange("p m o t -> p (m o t)"),
+        )
+        for s in range(S):
+            for k in range(K):
+                nc.sync.dma_start(
+                    out=w_mx[s][s * (P // S) : (s + 1) * (P // S), k, :],
+                    in_=w_all[k * (P // S) : (k + 1) * (P // S), :],
+                )
+        haar_rows(2)
         haar_cols(2)
         square(2)
         add_up(mean_ps, sums, 2)
+        haar_cols(3)
+        square(3)
+        add_up(mean_ps, sums, 3)
         add_up(meansq_ps, sumsq, 2)
-        for n in (3, 4):
-            haar_cols(n)
-            square(n)
-            add_up(mean_ps, sums, n)
-        for n in (3, 4):
-            add_up(meansq_ps, sumsq, n)
-
-        w_all = keep.tile([P, K, CO], I32, align_bytes=64)
-        w_scales = keep.tile([P, K, CO], U8, align_bytes=64)
-        nc.vector.quantize_mx(
-            out=w_all[:].rearrange("p n o -> p (n o)").bitcast(FP8X4),
-            scales=w_scales[:].rearrange("p n o -> p (n o)"),
-            in_=w_grouped[:].rearrange("p n m o t -> p (n m o t)"),
-        )
+        haar_cols(4)
+        square(4)
+        add_up(mean_ps, sums, 4)
+        add_up(meansq_ps, sumsq, 3)
+        add_up(meansq_ps, sumsq, 4)
+        warm = psum.tile([P, CO], F32, tag="acc5", name="warm")
+        for i in range(WARM_PASSES):
+            nc.tensor.matmul_mx(
+                out=warm[:],
+                lhsT=w_all[:, 0:P].bitcast(FP8X4),
+                lhsT_scale=w_all[:, CO:].bitcast(U8)[:, 0:P],
+                rhs=w_all[:, 0:CO].bitcast(FP8X4),
+                rhs_scale=w_all[:, CO:].bitcast(U8),
+                start=True,
+                stop=True,
+            )
 
         mean = keep.tile([P, K], F32)
         nc.vector.tensor_copy(out=mean[:], in_=mean_ps[:])
@@ -268,9 +271,6 @@ def tile_hwdconv_s_kernel(tc, x, gn_scale, gn_bias, w_proj, out):
         rstd = keep.tile([P, K], F32)
         slope = keep.tile([P, K, T], F32)
         offset = keep.tile([P, K, T], F32)
-        nc.vector.tensor_copy(
-            out=w_codes[0][0 : P // S, :, :], in_=w_all[0 : P // S, :, :]
-        )
         for k in range(K):
             nc.scalar.activation(
                 out=rstd[:, k : k + 1], in_=meansq_ps[:, k : k + 1],
@@ -309,9 +309,6 @@ def tile_hwdconv_s_kernel(tc, x, gn_scale, gn_bias, w_proj, out):
             for k in range(K):
                 for t in range(T):
                     normalise(nc.scalar if t % 2 == 0 else nc.vector, piece, k, t)
-        nc.vector.tensor_copy(
-            out=w_codes[1][P // S : P, :, :], in_=w_all[P // S : P, :, :]
-        )
 
         y_grouped = keep.tile([P, N_TILES, K, N_PIX, T], BF16, align_bytes=64)
         y_codes = keep.tile([P, N_TILES, K, N_PIX], I32, align_bytes=64)
@@ -319,15 +316,17 @@ def tile_hwdconv_s_kernel(tc, x, gn_scale, gn_bias, w_proj, out):
         out_dram = out.rearrange("(m o) (s i) j -> m o s (i j)", o=P, s=S)
 
         def regroup(n):
-            nc.vector.tensor_copy(
+            copy = nc.scalar.copy if n == N_TILES - 1 else nc.vector.tensor_copy
+            copy(
                 out=y_grouped[:, n, :, :, :].rearrange("p k (c i) t -> p (k c) t i", i=RUN),
                 in_=y_planar[:, n, :, :, :].rearrange("p t k (c i) -> p (k c) t i", i=RUN),
             )
 
         regroup(0)
+        regroup(N_TILES - 1)
         for n in range(N_TILES):
             px = slice(n * N_PIX, (n + 1) * N_PIX)
-            if n + 1 < N_TILES:
+            if n + 2 < N_TILES:
                 regroup(n + 1)
             nc.vector.quantize_mx(
                 out=y_codes[:, n, :, :].rearrange("p k c -> p (k c)").bitcast(FP8X4),
@@ -340,12 +339,11 @@ def tile_hwdconv_s_kernel(tc, x, gn_scale, gn_bias, w_proj, out):
                 )
                 for s in range(S):
                     for k in range(K):
-                        col = k if s == 0 else 1 - k
                         o_cols = slice(m * P, (m + 1) * P)
                         nc.tensor.matmul_mx(
                             out=acc[:, s, :],
-                            lhsT=w_codes[s][:, col, o_cols].bitcast(FP8X4),
-                            lhsT_scale=w_scales[:, col, o_cols],
+                            lhsT=w_mx[s][:, k, o_cols].bitcast(FP8X4),
+                            lhsT_scale=w_mx[s][:, k, CO:].bitcast(U8)[:, o_cols],
                             rhs=y_codes[:, n, k, :].bitcast(FP8X4),
                             rhs_scale=y_scales[:, n, k, :],
                             start=k == 0,

@@ -59,14 +59,20 @@ def tile_hwdconv_s_kernel(tc, x, gn_scale, gn_bias, w_proj, out):
             keep.tile([P, T, rows // 2, 2, W], BF16, name="x_sb%d" % i)
             for i, rows in enumerate(CHUNK_ROWS)
         ]
-        for i, (row0, row1) in enumerate(chunks):
-            cols = slice(row0 * W, row1 * W)
-            x_flat = x_sb[i][:].rearrange("p t i a w -> p t (i a w)")
+
+        def load(queue, i, s):
+            cols = slice(chunks[i][0] * W, chunks[i][1] * W)
             for r in range(R):
-                for s in range(S):
-                    queue = nc.scalar if s == 1 and i < 2 else nc.sync
-                    p0 = (s * R + r) * Q
-                    queue.dma_start(out=x_flat[p0 : p0 + Q, :, :], in_=x_dram[s][:, :, cols])
+                p0 = (s * R + r) * Q
+                queue.dma_start(
+                    out=x_sb[i][p0 : p0 + Q, :, :, :, :].rearrange("p t i a w -> p t (i a w)"),
+                    in_=x_dram[s][:, :, cols],
+                )
+
+        for i in range(len(chunks)):
+            load(nc.sync, i, 0)
+            if i < 2:
+                load(nc.scalar, i, 1)
         gn_rows = keep.tile([P, S, R * C], BF16)
         nc.vector.memset(gn_rows[:], 0.0)
         ident = keep.tile([P, P], BF16)
@@ -187,6 +193,7 @@ def tile_hwdconv_s_kernel(tc, x, gn_scale, gn_bias, w_proj, out):
         )
         nc.tensor.matmul(out=shift_ps[:], lhsT=pair_2d, rhs=est[:, 1:3], start=False, stop=True)
         nc.scalar.mul(out=shift[:], in_=shift_ps[:], mul=float(HALF_ROWS // chunks[0][1]))
+        load(nc.scalar, 2, 1)
 
         haar_rows(1)
 
@@ -213,6 +220,11 @@ def tile_hwdconv_s_kernel(tc, x, gn_scale, gn_bias, w_proj, out):
             add_up(mean_ps, sums, n)
             add_up(meansq_ps, sumsq, n)
 
+        haar_rows(2)
+        haar_cols(2)
+        square(2)
+        add_up(mean_ps, sums, 2)
+
         w_all = keep.tile([P, CO + CO // 4], I32, align_bytes=64)
         nc.vector.quantize_mx(
             out=w_all[:, 0:CO].bitcast(FP8X4),
@@ -225,10 +237,6 @@ def tile_hwdconv_s_kernel(tc, x, gn_scale, gn_bias, w_proj, out):
                     out=w_mx[s][s * (P // S) : (s + 1) * (P // S), k, :],
                     in_=w_all[k * (P // S) : (k + 1) * (P // S), :],
                 )
-        haar_rows(2)
-        haar_cols(2)
-        square(2)
-        add_up(mean_ps, sums, 2)
         haar_cols(3)
         square(3)
         add_up(mean_ps, sums, 3)

@@ -115,7 +115,7 @@ def tile_hwdconv_s_kernel(tc, x, gn_scale, gn_bias, w_proj, out):
         pair_2d = pair[:].rearrange("p s j -> p (s j)")
 
         u = [
-            keep.tile([P, T * (rows // 2), HALF_W, 2], F32, name="u%d" % i)
+            keep.tile([P, 2, T * (rows // 2), HALF_W], F32, name="u%d" % i)
             for i, rows in enumerate(CHUNK_ROWS)
         ]
         bands = keep.tile([P, K, T, PIX], F32)
@@ -127,15 +127,16 @@ def tile_hwdconv_s_kernel(tc, x, gn_scale, gn_bias, w_proj, out):
         shift = keep.tile([P, K], F32)
 
         def haar_rows(i):
-            rows = x_sb[i][:].rearrange("p t i a w -> p (t i) a w")
-            nc.vector.scalar_tensor_tensor(
-                out=u[i][:].rearrange("p i j b -> p i (j b)"),
-                in0=rows[:, :, 0, :],
-                scalar=row_sign[:, 0:1],
-                in1=rows[:, :, 1, :],
-                op0=ALU.mult,
-                op1=ALU.add,
-            )
+            rows = x_sb[i][:].rearrange("p t i a (j b) -> p (t i) a j b", b=2)
+            for b in range(2):
+                nc.vector.scalar_tensor_tensor(
+                    out=u[i][:, b, :, :],
+                    in0=rows[:, :, 0, :, b],
+                    scalar=row_sign[:, 0:1],
+                    in1=rows[:, :, 1, :, b],
+                    op0=ALU.mult,
+                    op1=ALU.add,
+                )
 
         def piece_pixels(n):
             i, pair0, pair1 = PIECES[n]
@@ -144,15 +145,15 @@ def tile_hwdconv_s_kernel(tc, x, gn_scale, gn_bias, w_proj, out):
 
         def haar_cols(n):
             i, pair0, pair1 = PIECES[n]
-            u_px = u[i][:].rearrange("p (t i) j b -> p t (i j) b", t=T)
-            u_px = u_px[:, :, pair0 * HALF_W : pair1 * HALF_W, :]
+            u_px = u[i][:].rearrange("p b (t i) j -> p b t (i j)", t=T)
+            u_px = u_px[:, :, :, pair0 * HALF_W : pair1 * HALF_W]
             px = piece_pixels(n)
             for k in range(K):
                 nc.vector.scalar_tensor_tensor(
                     out=bands[:, k, :, px],
-                    in0=u_px[:, :, :, 1],
+                    in0=u_px[:, 1, :, :],
                     scalar=shift[:, k : k + 1],
-                    in1=u_px[:, :, :, 0],
+                    in1=u_px[:, 0, :, :],
                     op0=ALU.subtract,
                     op1=ALU.subtract if k else ALU.add,
                     accum_out=sums[:, n, k : k + 1],
@@ -181,7 +182,7 @@ def tile_hwdconv_s_kernel(tc, x, gn_scale, gn_bias, w_proj, out):
         for n, (b, sign) in enumerate(((1, 1.0), (0, 1.0), (0, -1.0))):
             nc.scalar.activation(
                 out=est_scrap[:, n, :, :],
-                in_=u[0][:, :, :, b],
+                in_=u[0][:, b, :, :],
                 func=ACT.Copy,
                 scale=sign,
                 accum_out=est[:, n : n + 1],

@@ -27,8 +27,8 @@ CO = 256
 M_TILES = CO // P
 EPS = 1e-5
 
-CHUNK_ROWS = (4, 12, 16)
-PIECES = ((0, 0, 2), (1, 0, 6), (2, 0, 4), (2, 4, 7), (2, 7, 8))
+CHUNK_ROWS = (4, 12, 12, 4)
+PIECES = ((0, 0, 2), (1, 0, 6), (2, 0, 6), (3, 0, 2))
 N_TILES = 4
 N_PIX = PIX // N_TILES
 NORM_PIECES = 2
@@ -162,12 +162,23 @@ def tile_hwdconv_s_kernel(tc, x, gn_scale, gn_bias, w_proj, out):
         def square(n):
             px = piece_pixels(n)
             for k in range(K):
-                nc.scalar.activation(
-                    out=squares_scrap[:, k, :, px],
-                    in_=bands[:, k, :, px],
-                    func=ACT.Square,
-                    accum_out=sumsq[:, n, k : k + 1],
-                )
+                if n == len(PIECES) - 1 and k == K - 1:
+                    nc.vector.scalar_tensor_tensor(
+                        out=squares_scrap[:, k, :, px],
+                        in0=bands[:, k, :, px],
+                        scalar=1.0,
+                        in1=bands[:, k, :, px],
+                        op0=ALU.mult,
+                        op1=ALU.mult,
+                        accum_out=sumsq[:, n, k : k + 1],
+                    )
+                else:
+                    nc.scalar.activation(
+                        out=squares_scrap[:, k, :, px],
+                        in_=bands[:, k, :, px],
+                        func=ACT.Square,
+                        accum_out=sumsq[:, n, k : k + 1],
+                    )
 
         def add_up(total_ps, parts, n):
             nc.tensor.matmul(
@@ -202,13 +213,15 @@ def tile_hwdconv_s_kernel(tc, x, gn_scale, gn_bias, w_proj, out):
         for m in range(M_TILES):
             for t in range(T):
                 nc.tensor.transpose(w_t[:, m, t, :], w_sb[:, m, t : t + T * (P - 1) + 1 : T], ident[:])
-        w_grouped = keep.tile([P, M_TILES, P, T], BF16, align_bytes=64)
-        nc.scalar.copy(out=w_grouped[:], in_=w_t[:].rearrange("p m t o -> p m o t"))
 
         haar_cols(0)
         square(0)
+        load(nc.scalar, 3, 1)
         haar_cols(1)
         square(1)
+        w_grouped = keep.tile([P, M_TILES, P, T], BF16, align_bytes=64)
+        nc.scalar.copy(out=w_grouped[:], in_=w_t[:].rearrange("p m t o -> p m o t"))
+
         gn_t = psum.tile([P, T, P], BF16, tag="acc3", name="gn_t")
         gn_flat = gn_rows[:].rearrange("p s c -> p (s c)")
         for t in range(T):
@@ -220,7 +233,6 @@ def tile_hwdconv_s_kernel(tc, x, gn_scale, gn_bias, w_proj, out):
         for n in (0, 1):
             add_up(mean_ps, sums, n)
             add_up(meansq_ps, sumsq, n)
-
         haar_rows(2)
         haar_cols(2)
         square(2)
@@ -238,15 +250,12 @@ def tile_hwdconv_s_kernel(tc, x, gn_scale, gn_bias, w_proj, out):
                     out=w_mx[s][s * (P // S) : (s + 1) * (P // S), k, :],
                     in_=w_all[k * (P // S) : (k + 1) * (P // S), :],
                 )
+        haar_rows(3)
         haar_cols(3)
         square(3)
         add_up(mean_ps, sums, 3)
         add_up(meansq_ps, sumsq, 2)
-        haar_cols(4)
-        square(4)
-        add_up(mean_ps, sums, 4)
         add_up(meansq_ps, sumsq, 3)
-        add_up(meansq_ps, sumsq, 4)
         warm = psum.tile([P, CO], F32, tag="acc5", name="warm")
         for i in range(WARM_PASSES):
             nc.tensor.matmul_mx(

@@ -78,8 +78,9 @@ def tile_hwdconv_s_kernel(tc, x, gn_scale, gn_bias, w_proj, out):
         ident = keep.tile([P, P], BF16)
         make_identity(nc, ident[:])
         nc.gpsimd.dma_start(out=w_sb[:], in_=w_dram)
+        load(nc.gpsimd, 3, 1)
         for i, vec in enumerate((gn_scale, gn_bias)):
-            nc.gpsimd.dma_start(
+            nc.sync.dma_start(
                 out=gn_rows[i * K : (i + 1) * K, :, :],
                 in_=vec.rearrange("(k c) -> k c", k=K).unsqueeze(1).to_broadcast([K, S, R * C]),
             )
@@ -89,8 +90,12 @@ def tile_hwdconv_s_kernel(tc, x, gn_scale, gn_bias, w_proj, out):
         for s in range(S):
             p0 = (s * R + 1) * Q
             nc.vector.memset(row_sign[p0 : p0 + Q, :], -1.0)
+        col_sign = keep.tile([P, K], F32)
+        nc.vector.memset(col_sign[:, 0:1], 1.0)
+        nc.vector.memset(col_sign[:, 1:2], -1.0)
         table_warm = keep.tile([P, 1], F32)
         nc.scalar.activation(out=table_warm[:], in_=row_sign[:], func=ACT.Abs_reciprocal_sqrt)
+        load(nc.scalar, 2, 1)
 
         w_mx = [
             keep.tile([P, K, CO + CO // 4], I32, align_bytes=64, name="w_mx%d" % s)
@@ -125,6 +130,7 @@ def tile_hwdconv_s_kernel(tc, x, gn_scale, gn_bias, w_proj, out):
         mean_ps = psum.tile([P, K], F32, tag="mean", name="mean_ps")
         meansq_ps = psum.tile([P, K], F32, name="meansq_ps")
         shift = keep.tile([P, K], F32)
+        est = keep.tile([P, 2], F32)
 
         def haar_rows(i):
             rows = x_sb[i][:].rearrange("p t i a (j b) -> p (t i) a j b", b=2)
@@ -136,6 +142,7 @@ def tile_hwdconv_s_kernel(tc, x, gn_scale, gn_bias, w_proj, out):
                     in1=rows[:, :, 1, :, b],
                     op0=ALU.mult,
                     op1=ALU.add,
+                    accum_out=est[:, b : b + 1] if i == 0 else None,
                 )
 
         def piece_pixels(n):
@@ -187,25 +194,18 @@ def tile_hwdconv_s_kernel(tc, x, gn_scale, gn_bias, w_proj, out):
             )
 
         haar_rows(0)
-        est_rows = T * CHUNK_ROWS[0] // 2
-        est = keep.tile([P, 3], F32)
-        est_scrap = keep.tile([P, 3, est_rows, HALF_W], BF16)
-        for n, (b, sign) in enumerate(((1, 1.0), (0, 1.0), (0, -1.0))):
-            nc.scalar.activation(
-                out=est_scrap[:, n, :, :],
-                in_=u[0][:, b, :, :],
-                func=ACT.Copy,
-                scale=sign,
-                accum_out=est[:, n : n + 1],
-            )
-        shift_ps = psum.tile([P, K], F32, tag="mean", name="shift_ps")
-        nc.tensor.matmul(
-            out=shift_ps[:], lhsT=pair_2d, rhs=est[:, 0:1].to_broadcast([P, K]),
-            start=True, stop=False,
+        est_bands = keep.tile([P, K], F32)
+        nc.vector.scalar_tensor_tensor(
+            out=est_bands[:],
+            in0=col_sign[:],
+            scalar=est[:, 0:1],
+            in1=est[:, 1:2].to_broadcast([P, K]),
+            op0=ALU.mult,
+            op1=ALU.add,
         )
-        nc.tensor.matmul(out=shift_ps[:], lhsT=pair_2d, rhs=est[:, 1:3], start=False, stop=True)
+        shift_ps = psum.tile([P, K], F32, tag="mean", name="shift_ps")
+        nc.tensor.matmul(out=shift_ps[:], lhsT=pair_2d, rhs=est_bands[:], start=True, stop=True)
         nc.scalar.mul(out=shift[:], in_=shift_ps[:], mul=float(HALF_ROWS // chunks[0][1]))
-        load(nc.scalar, 2, 1)
 
         haar_rows(1)
 
@@ -214,29 +214,29 @@ def tile_hwdconv_s_kernel(tc, x, gn_scale, gn_bias, w_proj, out):
             for t in range(T):
                 nc.tensor.transpose(w_t[:, m, t, :], w_sb[:, m, t : t + T * (P - 1) + 1 : T], ident[:])
 
-        haar_cols(0)
-        square(0)
-        load(nc.scalar, 3, 1)
-        haar_cols(1)
-        square(1)
         w_grouped = keep.tile([P, M_TILES, P, T], BF16, align_bytes=64)
         nc.scalar.copy(out=w_grouped[:], in_=w_t[:].rearrange("p m t o -> p m o t"))
-
+        haar_cols(0)
+        square(0)
+        haar_cols(1)
+        square(1)
         gn_t = psum.tile([P, T, P], BF16, tag="acc3", name="gn_t")
         gn_flat = gn_rows[:].rearrange("p s c -> p (s c)")
         for t in range(T):
             nc.tensor.transpose(gn_t[:, t, :], gn_flat[:, t : t + T * (P - 1) + 1 : T], ident[:])
         gain = keep.tile([P, K, T], F32)
+        neg_gain = keep.tile([P, K, T], F32)
         bias = keep.tile([P, K, T], F32)
+        nc.scalar.activation(
+            out=neg_gain[:], in_=gn_t[:, :, 0:K].rearrange("p t k -> p k t"),
+            func=ACT.Copy, scale=-1.0,
+        )
         nc.scalar.copy(out=gain[:], in_=gn_t[:, :, 0:K].rearrange("p t k -> p k t"))
         nc.scalar.copy(out=bias[:], in_=gn_t[:, :, K : 2 * K].rearrange("p t k -> p k t"))
         for n in (0, 1):
             add_up(mean_ps, sums, n)
             add_up(meansq_ps, sumsq, n)
         haar_rows(2)
-        haar_cols(2)
-        square(2)
-        add_up(mean_ps, sums, 2)
 
         w_all = keep.tile([P, CO + CO // 4], I32, align_bytes=64)
         nc.vector.quantize_mx(
@@ -250,11 +250,15 @@ def tile_hwdconv_s_kernel(tc, x, gn_scale, gn_bias, w_proj, out):
                     out=w_mx[s][s * (P // S) : (s + 1) * (P // S), k, :],
                     in_=w_all[k * (P // S) : (k + 1) * (P // S), :],
                 )
+        haar_cols(2)
+        square(2)
+        add_up(mean_ps, sums, 2)
+
         haar_rows(3)
         haar_cols(3)
         square(3)
-        add_up(mean_ps, sums, 3)
         add_up(meansq_ps, sumsq, 2)
+        add_up(mean_ps, sums, 3)
         add_up(meansq_ps, sumsq, 3)
         warm = psum.tile([P, CO], F32, tag="acc5", name="warm")
         for i in range(WARM_PASSES):
@@ -268,31 +272,26 @@ def tile_hwdconv_s_kernel(tc, x, gn_scale, gn_bias, w_proj, out):
                 stop=True,
             )
 
-        mean = keep.tile([P, K], F32)
-        nc.vector.tensor_copy(out=mean[:], in_=mean_ps[:])
         pull = keep.tile([P, K, T], F32)
-        nc.vector.scalar_tensor_tensor(
-            out=pull[:],
-            in0=gain[:],
-            scalar=-1.0,
-            in1=mean[:].unsqueeze(2).to_broadcast([P, K, T]),
-            op0=ALU.mult,
-            op1=ALU.mult,
-        )
-        mean_squared = keep.tile([P, K], F32)
-        nc.vector.tensor_tensor(out=mean_squared[:], in0=mean[:], in1=mean[:], op=ALU.mult)
         eps_pull = keep.tile([P, K], F32)
-        nc.vector.tensor_scalar(
-            out=eps_pull[:], in0=mean_squared[:],
-            scalar1=-1.0, scalar2=EPS_UNHALVED, op0=ALU.mult, op1=ALU.add,
-        )
+        for k in range(K):
+            nc.vector.tensor_scalar(
+                out=eps_pull[:, k : k + 1], in0=mean_ps[:, k : k + 1],
+                scalar1=mean_ps[:, k : k + 1], scalar2=EPS_UNHALVED,
+                op0=ALU.mult, op1=ALU.subtract,
+            )
+        for k in range(K):
+            nc.vector.tensor_scalar(
+                out=pull[:, k, :], in0=neg_gain[:, k, :],
+                scalar1=mean_ps[:, k : k + 1], scalar2=None, op0=ALU.mult,
+            )
         rstd = keep.tile([P, K], F32)
         slope = keep.tile([P, K, T], F32)
         offset = keep.tile([P, K, T], F32)
         for k in range(K):
             nc.scalar.activation(
                 out=rstd[:, k : k + 1], in_=meansq_ps[:, k : k + 1],
-                func=ACT.Abs_reciprocal_sqrt, bias=eps_pull[:, k : k + 1],
+                func=ACT.Abs_reciprocal_sqrt, scale=-1.0, bias=eps_pull[:, k : k + 1],
             )
         for k in range(K):
             nc.vector.tensor_scalar(

@@ -77,8 +77,7 @@ def tile_hwdconv_s_kernel(tc, x, gn_scale, gn_bias, w_proj, out):
         nc.vector.memset(gn_rows[:], 0.0)
         ident = keep.tile([P, P], BF16)
         make_identity(nc, ident[:])
-        nc.gpsimd.dma_start(out=w_sb[:], in_=w_dram)
-        load(nc.gpsimd, 3, 1)
+        load(nc.sync, 3, 1)
         for i, vec in enumerate((gn_scale, gn_bias)):
             nc.sync.dma_start(
                 out=gn_rows[i * K : (i + 1) * K, :, :],
@@ -95,6 +94,7 @@ def tile_hwdconv_s_kernel(tc, x, gn_scale, gn_bias, w_proj, out):
         nc.vector.memset(col_sign[:, 1:2], -1.0)
         table_warm = keep.tile([P, 1], F32)
         nc.scalar.activation(out=table_warm[:], in_=row_sign[:], func=ACT.Abs_reciprocal_sqrt)
+        nc.scalar.dma_start(out=w_sb[:], in_=w_dram)
         load(nc.scalar, 2, 1)
 
         w_mx = [

@@ -69,33 +69,34 @@ def tile_hwdconv_s_kernel(tc, x, gn_scale, gn_bias, w_proj, out):
                     in_=x_dram[s][:, :, cols],
                 )
 
-        for i in range(len(chunks)):
+        for i in range(2):
             load(nc.sync, i, 0)
-            if i < 2:
-                load(nc.scalar, i, 1)
-        gn_rows = keep.tile([P, S, R * C], BF16)
-        nc.vector.memset(gn_rows[:], 0.0)
+            load(nc.scalar, i, 1)
+        row_sign = keep.tile([P, 1], F32)
+        nc.vector.memset(row_sign[:], 1.0)
+        for s in range(S):
+            p0 = (s * R + 1) * Q
+            nc.vector.memset(row_sign[p0 : p0 + Q, :], -1.0)
+        table_warm = keep.tile([P, 1], F32)
+        nc.scalar.activation(out=table_warm[:], in_=row_sign[:], func=ACT.Abs_reciprocal_sqrt)
+        nc.sync.dma_start(out=w_sb[:], in_=w_dram)
+        load(nc.sync, 2, 0)
+        load(nc.scalar, 2, 1)
+        load(nc.sync, 3, 0)
+        load(nc.sync, 3, 1)
         ident = keep.tile([P, P], BF16)
         make_identity(nc, ident[:])
-        load(nc.sync, 3, 1)
+        gn_rows = keep.tile([P, S, R * C], BF16)
+        nc.gpsimd.memset(gn_rows[:], 0.0)
         for i, vec in enumerate((gn_scale, gn_bias)):
             nc.sync.dma_start(
                 out=gn_rows[i * K : (i + 1) * K, :, :],
                 in_=vec.rearrange("(k c) -> k c", k=K).unsqueeze(1).to_broadcast([K, S, R * C]),
             )
 
-        row_sign = keep.tile([P, 1], F32)
-        nc.vector.memset(row_sign[:], 1.0)
-        for s in range(S):
-            p0 = (s * R + 1) * Q
-            nc.vector.memset(row_sign[p0 : p0 + Q, :], -1.0)
         col_sign = keep.tile([P, K], F32)
         nc.vector.memset(col_sign[:, 0:1], 1.0)
         nc.vector.memset(col_sign[:, 1:2], -1.0)
-        table_warm = keep.tile([P, 1], F32)
-        nc.scalar.activation(out=table_warm[:], in_=row_sign[:], func=ACT.Abs_reciprocal_sqrt)
-        nc.scalar.dma_start(out=w_sb[:], in_=w_dram)
-        load(nc.scalar, 2, 1)
 
         w_mx = [
             keep.tile([P, K, CO + CO // 4], I32, align_bytes=64, name="w_mx%d" % s)
@@ -103,7 +104,7 @@ def tile_hwdconv_s_kernel(tc, x, gn_scale, gn_bias, w_proj, out):
         ]
         for s in range(S):
             p0 = (1 - s) * (P // S)
-            nc.vector.memset(w_mx[s][p0 : p0 + P // S, :, :], 0)
+            nc.gpsimd.memset(w_mx[s][p0 : p0 + P // S, :, :], 0)
 
         pair_half = keep.tile([P, P // S], F32)
         nc.vector.tensor_tensor(
@@ -236,7 +237,6 @@ def tile_hwdconv_s_kernel(tc, x, gn_scale, gn_bias, w_proj, out):
         for n in (0, 1):
             add_up(mean_ps, sums, n)
             add_up(meansq_ps, sumsq, n)
-        haar_rows(2)
 
         w_all = keep.tile([P, CO + CO // 4], I32, align_bytes=64)
         nc.vector.quantize_mx(
@@ -250,6 +250,8 @@ def tile_hwdconv_s_kernel(tc, x, gn_scale, gn_bias, w_proj, out):
                     out=w_mx[s][s * (P // S) : (s + 1) * (P // S), k, :],
                     in_=w_all[k * (P // S) : (k + 1) * (P // S), :],
                 )
+        haar_rows(2)
+
         haar_cols(2)
         square(2)
         add_up(mean_ps, sums, 2)

@@ -33,7 +33,8 @@ N_TILES = 4
 N_PIX = PIX // N_TILES
 NORM_PIECES = 2
 NORM_PIX = PIX // NORM_PIECES
-WARM_PASSES = 12
+WARM_EARLY = 8
+WARM_LATE = 22
 RUN = 4
 
 EPS_UNHALVED = 4.0 * EPS
@@ -238,6 +239,8 @@ def tile_hwdconv_s_kernel(tc, x, gn_scale, gn_bias, w_proj, out):
             add_up(mean_ps, sums, n)
             add_up(meansq_ps, sumsq, n)
 
+        haar_rows(2)
+
         w_all = keep.tile([P, CO + CO // 4], I32, align_bytes=64)
         nc.vector.quantize_mx(
             out=w_all[:, 0:CO].bitcast(FP8X4),
@@ -250,8 +253,22 @@ def tile_hwdconv_s_kernel(tc, x, gn_scale, gn_bias, w_proj, out):
                     out=w_mx[s][s * (P // S) : (s + 1) * (P // S), k, :],
                     in_=w_all[k * (P // S) : (k + 1) * (P // S), :],
                 )
-        haar_rows(2)
 
+        warm = psum.tile([P, CO], F32, tag="acc5", name="warm")
+
+        def keep_warm(passes):
+            for i in range(passes):
+                nc.tensor.matmul_mx(
+                    out=warm[:],
+                    lhsT=w_all[:, 0:P].bitcast(FP8X4),
+                    lhsT_scale=w_all[:, CO:].bitcast(U8)[:, 0:P],
+                    rhs=w_all[:, 0:CO].bitcast(FP8X4),
+                    rhs_scale=w_all[:, CO:].bitcast(U8),
+                    start=True,
+                    stop=True,
+                )
+
+        keep_warm(WARM_EARLY)
         haar_cols(2)
         square(2)
         add_up(mean_ps, sums, 2)
@@ -262,17 +279,7 @@ def tile_hwdconv_s_kernel(tc, x, gn_scale, gn_bias, w_proj, out):
         add_up(meansq_ps, sumsq, 2)
         add_up(mean_ps, sums, 3)
         add_up(meansq_ps, sumsq, 3)
-        warm = psum.tile([P, CO], F32, tag="acc5", name="warm")
-        for i in range(WARM_PASSES):
-            nc.tensor.matmul_mx(
-                out=warm[:],
-                lhsT=w_all[:, 0:P].bitcast(FP8X4),
-                lhsT_scale=w_all[:, CO:].bitcast(U8)[:, 0:P],
-                rhs=w_all[:, 0:CO].bitcast(FP8X4),
-                rhs_scale=w_all[:, CO:].bitcast(U8),
-                start=True,
-                stop=True,
-            )
+        keep_warm(WARM_LATE)
 
         pull = keep.tile([P, K, T], F32)
         eps_pull = keep.tile([P, K], F32)

from contextlib import ExitStack

import concourse.mybir as mybir
from concourse.masks import make_identity

F32 = mybir.dt.float32
BF16 = mybir.dt.bfloat16
I32 = mybir.dt.int32
U8 = mybir.dt.uint8
FP8X4 = mybir.dt.float8_e4m3fn_x4
ALU = mybir.AluOpType
ACT = mybir.ActivationFunctionType

P = 128
C = 128
H = 64
W = 64
T = 4
Q = C // T
S = 2
R = 2
K = 2
HALF_ROWS = H // S
HALF_W = W // 2
PIX = (HALF_ROWS // 2) * HALF_W
CO = 256
M_TILES = CO // P
EPS = 1e-5

CHUNK_ROWS = (4, 12, 12, 4)
PIECES = ((0, 0, 2), (1, 0, 6), (2, 0, 6), (3, 0, 2))
N_TILES = 4
N_PIX = PIX // N_TILES
NORM_PIECES = 2
NORM_PIX = PIX // NORM_PIECES
WARM_EARLY = 8
WARM_LATE = 22
RUN = 4

EPS_UNHALVED = 4.0 * EPS

FLOPS = 2 * CO * 4 * C * S * PIX


def tile_hwdconv_s_kernel(tc, x, gn_scale, gn_bias, w_proj, out):
    nc = tc.nc
    with ExitStack() as ctx:
        keep = ctx.enter_context(tc.tile_pool(name="keep", bufs=1))
        psum = ctx.enter_context(tc.psum_pool(name="psum", bufs=1))
        ctx.enter_context(tc.manual_schedule())

        x_dram = x.rearrange("(q t) (s h) w -> s q t (h w)", t=T, s=S)
        w_sb = keep.tile([P, M_TILES, K * R * C], BF16)
        w_dram = w_proj.rearrange("(m o) c -> o m c", o=P)
        bounds = [0]
        for rows in CHUNK_ROWS:
            bounds.append(bounds[-1] + rows)
        chunks = list(zip(bounds[:-1], bounds[1:]))
        x_sb = [
            keep.tile([P, T, rows // 2, 2, W], BF16, name="x_sb%d" % i)
            for i, rows in enumerate(CHUNK_ROWS)
        ]

        def load(queue, i, s):
            cols = slice(chunks[i][0] * W, chunks[i][1] * W)
            for r in range(R):
                p0 = (s * R + r) * Q
                queue.dma_start(
                    out=x_sb[i][p0 : p0 + Q, :, :, :, :].rearrange("p t i a w -> p t (i a w)"),
                    in_=x_dram[s][:, :, cols],
                )

        for i in range(2):
            load(nc.sync, i, 0)
            load(nc.scalar, i, 1)
        row_sign = keep.tile([P, 1], F32)
        nc.vector.memset(row_sign[:], 1.0)
        for s in range(S):
            p0 = (s * R + 1) * Q
            nc.vector.memset(row_sign[p0 : p0 + Q, :], -1.0)
        table_warm = keep.tile([P, 1], F32)
        nc.scalar.activation(out=table_warm[:], in_=row_sign[:], func=ACT.Abs_reciprocal_sqrt)
        nc.sync.dma_start(out=w_sb[:], in_=w_dram)
        load(nc.sync, 2, 0)
        load(nc.scalar, 2, 1)
        load(nc.sync, 3, 0)
        load(nc.sync, 3, 1)
        ident = keep.tile([P, P], BF16)
        make_identity(nc, ident[:])
        gn_rows = keep.tile([P, S, R * C], BF16)
        nc.gpsimd.memset(gn_rows[:], 0.0)
        for i, vec in enumerate((gn_scale, gn_bias)):
            nc.sync.dma_start(
                out=gn_rows[i * K : (i + 1) * K, :, :],
                in_=vec.rearrange("(k c) -> k c", k=K).unsqueeze(1).to_broadcast([K, S, R * C]),
            )

        col_sign = keep.tile([P, K], F32)
        nc.vector.memset(col_sign[:, 0:1], 1.0)
        nc.vector.memset(col_sign[:, 1:2], -1.0)

        w_mx = [
            keep.tile([P, K, CO + CO // 4], I32, align_bytes=64, name="w_mx%d" % s)
            for s in range(S)
        ]
        for s in range(S):
            p0 = (1 - s) * (P // S)
            nc.gpsimd.memset(w_mx[s][p0 : p0 + P // S, :, :], 0)

        pair_half = keep.tile([P, P // S], F32)
        nc.vector.tensor_tensor(
            out=pair_half[:], in0=ident[:, 0 : P // S], in1=ident[:, P // S : P], op=ALU.add
        )
        pair = keep.tile([P, S, P // S], F32)
        nc.vector.tensor_scalar(
            out=pair[:],
            in0=pair_half[:].unsqueeze(1).to_broadcast([P, S, P // S]),
            scalar1=1.0 / (T * S * PIX),
            scalar2=None,
            op0=ALU.mult,
        )
        pair_2d = pair[:].rearrange("p s j -> p (s j)")

        u = [
            keep.tile([P, 2, T * (rows // 2), HALF_W], F32, name="u%d" % i)
            for i, rows in enumerate(CHUNK_ROWS)
        ]
        bands = keep.tile([P, K, T, PIX], F32)
        squares_scrap = keep.tile([P, K, T, PIX], BF16)
        sums = keep.tile([P, len(PIECES), K], F32)
        sumsq = keep.tile([P, len(PIECES), K], F32)
        mean_ps = psum.tile([P, K], F32, tag="mean", name="mean_ps")
        meansq_ps = psum.tile([P, K], F32, name="meansq_ps")
        shift = keep.tile([P, K], F32)
        est = keep.tile([P, 2], F32)

        def haar_rows(i):
            rows = x_sb[i][:].rearrange("p t i a (j b) -> p (t i) a j b", b=2)
            for b in range(2):
                nc.vector.scalar_tensor_tensor(
                    out=u[i][:, b, :, :],
                    in0=rows[:, :, 0, :, b],
                    scalar=row_sign[:, 0:1],
                    in1=rows[:, :, 1, :, b],
                    op0=ALU.mult,
                    op1=ALU.add,
                    accum_out=est[:, b : b + 1] if i == 0 else None,
                )

        def piece_pixels(n):
            i, pair0, pair1 = PIECES[n]
            base = chunks[i][0] // 2
            return slice((base + pair0) * HALF_W, (base + pair1) * HALF_W)

        def haar_cols(n):
            i, pair0, pair1 = PIECES[n]
            u_px = u[i][:].rearrange("p b (t i) j -> p b t (i j)", t=T)
            u_px = u_px[:, :, :, pair0 * HALF_W : pair1 * HALF_W]
            px = piece_pixels(n)
            for k in range(K):
                nc.vector.scalar_tensor_tensor(
                    out=bands[:, k, :, px],
                    in0=u_px[:, 1, :, :],
                    scalar=shift[:, k : k + 1],
                    in1=u_px[:, 0, :, :],
                    op0=ALU.subtract,
                    op1=ALU.subtract if k else ALU.add,
                    accum_out=sums[:, n, k : k + 1],
                )

        def square(n):
            px = piece_pixels(n)
            for k in range(K):
                if n == len(PIECES) - 1 and k == K - 1:
                    nc.vector.scalar_tensor_tensor(
                        out=squares_scrap[:, k, :, px],
                        in0=bands[:, k, :, px],
                        scalar=1.0,
                        in1=bands[:, k, :, px],
                        op0=ALU.mult,
                        op1=ALU.mult,
                        accum_out=sumsq[:, n, k : k + 1],
                    )
                else:
                    nc.scalar.activation(
                        out=squares_scrap[:, k, :, px],
                        in_=bands[:, k, :, px],
                        func=ACT.Square,
                        accum_out=sumsq[:, n, k : k + 1],
                    )

        def add_up(total_ps, parts, n):
            nc.tensor.matmul(
                out=total_ps[:], lhsT=pair_2d, rhs=parts[:, n, :],
                start=n == 0, stop=n == len(PIECES) - 1,
            )

        haar_rows(0)
        est_bands = keep.tile([P, K], F32)
        nc.vector.scalar_tensor_tensor(
            out=est_bands[:],
            in0=col_sign[:],
            scalar=est[:, 0:1],
            in1=est[:, 1:2].to_broadcast([P, K]),
            op0=ALU.mult,
            op1=ALU.add,
        )
        shift_ps = psum.tile([P, K], F32, tag="mean", name="shift_ps")
        nc.tensor.matmul(out=shift_ps[:], lhsT=pair_2d, rhs=est_bands[:], start=True, stop=True)
        nc.scalar.mul(out=shift[:], in_=shift_ps[:], mul=float(HALF_ROWS // chunks[0][1]))

        haar_rows(1)

        w_t = psum.tile([P, M_TILES, T, P], BF16, tag="acc4", name="w_t")
        for m in range(M_TILES):
            for t in range(T):
                nc.tensor.transpose(w_t[:, m, t, :], w_sb[:, m, t : t + T * (P - 1) + 1 : T], ident[:])

        w_grouped = keep.tile([P, M_TILES, P, T], BF16, align_bytes=64)
        nc.scalar.copy(out=w_grouped[:], in_=w_t[:].rearrange("p m t o -> p m o t"))
        haar_cols(0)
        square(0)
        haar_cols(1)
        square(1)
        gn_t = psum.tile([P, T, P], BF16, tag="acc3", name="gn_t")
        gn_flat = gn_rows[:].rearrange("p s c -> p (s c)")
        for t in range(T):
            nc.tensor.transpose(gn_t[:, t, :], gn_flat[:, t : t + T * (P - 1) + 1 : T], ident[:])
        gain = keep.tile([P, K, T], F32)
        neg_gain = keep.tile([P, K, T], F32)
        bias = keep.tile([P, K, T], F32)
        nc.scalar.activation(
            out=neg_gain[:], in_=gn_t[:, :, 0:K].rearrange("p t k -> p k t"),
            func=ACT.Copy, scale=-1.0,
        )
        nc.scalar.copy(out=gain[:], in_=gn_t[:, :, 0:K].rearrange("p t k -> p k t"))
        nc.scalar.copy(out=bias[:], in_=gn_t[:, :, K : 2 * K].rearrange("p t k -> p k t"))
        for n in (0, 1):
            add_up(mean_ps, sums, n)
            add_up(meansq_ps, sumsq, n)

        haar_rows(2)

        w_all = keep.tile([P, CO + CO // 4], I32, align_bytes=64)
        nc.vector.quantize_mx(
            out=w_all[:, 0:CO].bitcast(FP8X4),
            scales=w_all[:, CO:].bitcast(U8),
            in_=w_grouped[:].rearrange("p m o t -> p (m o t)"),
        )
        for s in range(S):
            for k in range(K):
                nc.sync.dma_start(
                    out=w_mx[s][s * (P // S) : (s + 1) * (P // S), k, :],
                    in_=w_all[k * (P // S) : (k + 1) * (P // S), :],
                )

        warm = psum.tile([P, CO], F32, tag="acc5", name="warm")

        def keep_warm(passes):
            for i in range(passes):
                nc.tensor.matmul_mx(
                    out=warm[:],
                    lhsT=w_all[:, 0:P].bitcast(FP8X4),
                    lhsT_scale=w_all[:, CO:].bitcast(U8)[:, 0:P],
                    rhs=w_all[:, 0:CO].bitcast(FP8X4),
                    rhs_scale=w_all[:, CO:].bitcast(U8),
                    start=True,
                    stop=True,
                )

        keep_warm(WARM_EARLY)
        haar_cols(2)
        square(2)
        add_up(mean_ps, sums, 2)

        haar_rows(3)
        haar_cols(3)
        square(3)
        add_up(meansq_ps, sumsq, 2)
        add_up(mean_ps, sums, 3)
        add_up(meansq_ps, sumsq, 3)
        keep_warm(WARM_LATE)

        pull = keep.tile([P, K, T], F32)
        eps_pull = keep.tile([P, K], F32)
        for k in range(K):
            nc.vector.tensor_scalar(
                out=eps_pull[:, k : k + 1], in0=mean_ps[:, k : k + 1],
                scalar1=mean_ps[:, k : k + 1], scalar2=EPS_UNHALVED,
                op0=ALU.mult, op1=ALU.subtract,
            )
        for k in range(K):
            nc.vector.tensor_scalar(
                out=pull[:, k, :], in0=neg_gain[:, k, :],
                scalar1=mean_ps[:, k : k + 1], scalar2=None, op0=ALU.mult,
            )
        rstd = keep.tile([P, K], F32)
        slope = keep.tile([P, K, T], F32)
        offset = keep.tile([P, K, T], F32)
        for k in range(K):
            nc.scalar.activation(
                out=rstd[:, k : k + 1], in_=meansq_ps[:, k : k + 1],
                func=ACT.Abs_reciprocal_sqrt, scale=-1.0, bias=eps_pull[:, k : k + 1],
            )
        for k in range(K):
            nc.vector.tensor_scalar(
                out=slope[:, k, :], in0=gain[:, k, :],
                scalar1=rstd[:, k : k + 1], scalar2=None, op0=ALU.mult,
            )
            nc.vector.scalar_tensor_tensor(
                out=offset[:, k, :], in0=pull[:, k, :], scalar=rstd[:, k : k + 1],
                in1=bias[:, k, :], op0=ALU.mult, op1=ALU.add,
            )

        y_planar = keep.tile([P, N_TILES, T, K, N_PIX], BF16)

        def normalise(engine, piece, k, t):
            tiles = slice(piece * NORM_PIX // N_PIX, (piece + 1) * NORM_PIX // N_PIX)
            src = bands[:, k, t, piece * NORM_PIX : (piece + 1) * NORM_PIX].rearrange(
                "p (n c) -> p n c", c=N_PIX
            )
            slope_t, offset_t = slope[:, k, t : t + 1], offset[:, k, t : t + 1]
            if engine is nc.scalar:
                nc.scalar.activation(
                    out=y_planar[:, tiles, t, k, :], in_=src,
                    func=ACT.Identity, scale=slope_t, bias=offset_t,
                )
            else:
                nc.vector.tensor_scalar(
                    out=y_planar[:, tiles, t, k, :], in0=src,
                    scalar1=slope_t, scalar2=offset_t, op0=ALU.mult, op1=ALU.add,
                )

        for piece in range(NORM_PIECES):
            for k in range(K):
                for t in range(T):
                    normalise(nc.scalar if t % 2 == 0 else nc.vector, piece, k, t)

        y_grouped = keep.tile([P, N_TILES, K, N_PIX, T], BF16, align_bytes=64)
        y_codes = keep.tile([P, N_TILES, K, N_PIX], I32, align_bytes=64)
        y_scales = keep.tile([P, N_TILES, K, N_PIX], U8, align_bytes=64)
        out_dram = out.rearrange("(m o) (s i) j -> m o s (i j)", o=P, s=S)

        def regroup(n):
            copy = nc.scalar.copy if n == N_TILES - 1 else nc.vector.tensor_copy
            copy(
                out=y_grouped[:, n, :, :, :].rearrange("p k (c i) t -> p (k c) t i", i=RUN),
                in_=y_planar[:, n, :, :, :].rearrange("p t k (c i) -> p (k c) t i", i=RUN),
            )

        regroup(0)
        regroup(N_TILES - 1)
        for n in range(N_TILES):
            px = slice(n * N_PIX, (n + 1) * N_PIX)
            if n + 2 < N_TILES:
                regroup(n + 1)
            nc.vector.quantize_mx(
                out=y_codes[:, n, :, :].rearrange("p k c -> p (k c)").bitcast(FP8X4),
                scales=y_scales[:, n, :, :].rearrange("p k c -> p (k c)"),
                in_=y_grouped[:, n, :, :, :].rearrange("p k c t -> p (k c t)"),
            )
            for m in range(M_TILES):
                acc = psum.tile(
                    [P, S, N_PIX], F32, tag="acc%d" % ((n * M_TILES + m) % 6), name="acc%d%d" % (n, m)
                )
                for s in range(S):
                    for k in range(K):
                        o_cols = slice(m * P, (m + 1) * P)
                        nc.tensor.matmul_mx(
                            out=acc[:, s, :],
                            lhsT=w_mx[s][:, k, o_cols].bitcast(FP8X4),
                            lhsT_scale=w_mx[s][:, k, CO:].bitcast(U8)[:, o_cols],
                            rhs=y_codes[:, n, k, :].bitcast(FP8X4),
                            rhs_scale=y_scales[:, n, k, :],
                            start=k == 0,
                            stop=k == K - 1,
                        )
                result = keep.tile([P, S, N_PIX], F32, name="result%d%d" % (n, m))
                if n == N_TILES - 1 and m == 0:
                    nc.vector.tensor_scalar_max(out=result[:], in0=acc[:], scalar1=0.0)
                else:
                    nc.scalar.activation(out=result[:], in_=acc[:], func=ACT.Relu)
                nc.sync.dma_start(out=out_dram[m][:, :, px], in_=result[:])
